import numpy as np
import ml_dtypes

BF16 = ml_dtypes.bfloat16


def bf(x):
    return np.asarray(x, np.float32).astype(BF16)


def f32(x):
    return np.asarray(x, np.float32)


def f64(x):
    return np.asarray(x).astype(np.float64)


def striped(idx):
    return np.tile(idx.reshape(-1, 16).T, (8, 1))


C, S, N = 1024, 2048, 512
EPS = 1e-5
BASE = 10000.0


def sinusoidal_pe(t, d):
    pos = np.arange(t, dtype=np.float32)[:, None]
    div = np.exp(np.arange(0, d, 2, dtype=np.float32) * np.float32(-np.log(BASE) / d))
    pe = np.zeros((t, d), np.float32)
    pe[:, 0::2] = np.sin(pos * div)
    pe[:, 1::2] = np.cos(pos * div)
    return pe


def setup_inputs():
    return {"table": f32(np.random.standard_normal((C, S))), "pe": f32(np.ascontiguousarray(sinusoidal_pe(N, C).T)), "gain": f32(1.0 + 0.1 * np.random.standard_normal((C, 1))), "bias": f32(0.1 * np.random.standard_normal((C, 1))), "offs": striped(np.random.permutation(np.tile(np.arange(S), 2))[:N])}


def reference(table, pe, gain, bias, offs):
    idx = offs[:16].T.reshape(-1)
    x = f64(table)[:, idx] + f64(pe)
    m = x.mean(axis=0, keepdims=True)
    v = np.square(x - m).mean(axis=0, keepdims=True)
    return (x - m) / np.sqrt(v + EPS) * f64(gain) + f64(bias)

@@ -1,0 +1,80 @@
+import concourse.masks as masks
+import concourse.mybir as mybir
+
+F32 = mybir.dt.float32
+U16 = mybir.dt.uint16
+ALU = mybir.AluOpType
+ACT = mybir.ActivationFunctionType
+
+P = 128
+C, S, N = 1024, 2048, 512
+BLOCKS = C // P
+EPS = 1e-5
+
+FLOPS = 8 * C * N
+
+
+def tile_decoderlm_kernel(tc, table, pe, gain, bias, offs, out):
+    nc = tc.nc
+    with (
+        tc.tile_pool(name="held", bufs=1) as held,
+        tc.psum_pool(name="psum", bufs=1) as psum,
+    ):
+        offsets = held.tile([P, N // 16], U16, name="offsets")
+        nc.sync.dma_start(offsets[:], offs)
+
+        pe_blocks = [held.tile([P, N], F32, name=f"pe{b}") for b in range(BLOCKS)]
+        table_blocks = [held.tile([P, S], F32, name=f"table{b}") for b in range(BLOCKS)]
+        for b in range(BLOCKS):
+            rows = slice(b * P, (b + 1) * P)
+            nc.sync.dma_start(pe_blocks[b][:], pe[rows, :])
+            nc.sync.dma_start(table_blocks[b][:], table[rows, :])
+
+        affine_rows = held.tile([2 * BLOCKS, P], F32, name="affine_rows")
+        nc.scalar.dma_start(affine_rows[:BLOCKS, :], gain.rearrange("(b p) o -> b (p o)", p=P))
+        nc.scalar.dma_start(affine_rows[BLOCKS:, :], bias.rearrange("(b p) o -> b (p o)", p=P))
+        identity = held.tile([2 * BLOCKS, 2 * BLOCKS], F32, name="identity")
+        masks.make_identity(nc, identity[:])
+        affine_ps = psum.tile([P, 2 * BLOCKS], F32, name="affine_ps")
+        nc.tensor.matmul(affine_ps[:], affine_rows[:], identity[:], start=True, stop=True)
+        affine = held.tile([P, 2 * BLOCKS], F32, name="affine")
+        nc.vector.tensor_copy(affine[:], affine_ps[:])
+
+        averager = held.tile([P, P], F32, name="averager")
+        nc.gpsimd.memset(averager[:], 1.0 / C)
+
+        mean_ps = psum.tile([P, N], F32, name="mean_ps")
+        x_blocks = [held.tile([P, N], F32, name=f"x{b}") for b in range(BLOCKS)]
+        for b in range(BLOCKS):
+            nc.vector.tensor_tensor(
+                x_blocks[b][:], table_blocks[b][:].indirect(offsets[:]), pe_blocks[b][:], ALU.add
+            )
+            nc.tensor.matmul(
+                mean_ps[:], averager[:], x_blocks[b][:], start=(b == 0), stop=(b == BLOCKS - 1)
+            )
+
+        var_ps = psum.tile([P, N], F32, name="var_ps")
+        centred_blocks = [held.tile([P, N], F32, name=f"centred{b}") for b in range(BLOCKS)]
+        for b in range(BLOCKS):
+            nc.vector.tensor_tensor(centred_blocks[b][:], x_blocks[b][:], mean_ps[:], ALU.subtract)
+            squared = held.tile([P, N], F32, name=f"squared{b}")
+            nc.scalar.activation(squared[:], centred_blocks[b][:], ACT.Square)
+            nc.tensor.matmul(
+                var_ps[:], averager[:], squared[:], start=(b == 0), stop=(b == BLOCKS - 1)
+            )
+
+        rstd = held.tile([P, N], F32, name="rstd")
+        nc.scalar.activation(rstd[:], var_ps[:], ACT.Abs_reciprocal_sqrt, bias=EPS)
+
+        for b in range(BLOCKS):
+            normed = held.tile([P, N], F32, name=f"normed{b}")
+            nc.vector.tensor_tensor(normed[:], centred_blocks[b][:], rstd[:], ALU.mult)
+            result = held.tile([P, N], F32, name=f"result{b}")
+            nc.scalar.activation(
+                result[:],
+                normed[:],
+                ACT.Identity,
+                scale=affine[:, b : b + 1],
+                bias=affine[:, BLOCKS + b : BLOCKS + b + 1],
+            )
+            nc.sync.dma_start(out[b * P : (b + 1) * P, :], result[:])

@@ -42,30 +42,40 @@ def tile_decoderlm_kernel(tc, table, pe, gain, bias, offs, out):
 
         averager = held.tile([P, P], F32, name="averager")
         nc.gpsimd.memset(averager[:], 1.0 / C)
+        minus_block_averager = held.tile([P, P], F32, name="minus_block_averager")
+        nc.gpsimd.memset(minus_block_averager[:], -1.0 / P)
 
+        minus_k_ps = psum.tile([P, N], F32, name="minus_k_ps")
         mean_ps = psum.tile([P, N], F32, name="mean_ps")
-        x_blocks = [held.tile([P, N], F32, name=f"x{b}") for b in range(BLOCKS)]
-        for b in range(BLOCKS):
-            nc.vector.tensor_tensor(
-                x_blocks[b][:], table_blocks[b][:].indirect(offsets[:]), pe_blocks[b][:], ALU.add
-            )
-            nc.tensor.matmul(
-                mean_ps[:], averager[:], x_blocks[b][:], start=(b == 0), stop=(b == BLOCKS - 1)
-            )
-
         var_ps = psum.tile([P, N], F32, name="var_ps")
-        centred_blocks = [held.tile([P, N], F32, name=f"centred{b}") for b in range(BLOCKS)]
+        y_blocks = [held.tile([P, N], F32, name=f"y{b}") for b in range(BLOCKS)]
         for b in range(BLOCKS):
-            nc.vector.tensor_tensor(centred_blocks[b][:], x_blocks[b][:], mean_ps[:], ALU.subtract)
+            looked_up = table_blocks[b][:].indirect(offsets[:])
+            if b == 0:
+                x0 = held.tile([P, N], F32, name="x0")
+                nc.vector.tensor_tensor(x0[:], looked_up, pe_blocks[0][:], ALU.add)
+                nc.tensor.matmul(minus_k_ps[:], minus_block_averager[:], x0[:], start=True, stop=True)
+                nc.vector.tensor_tensor(y_blocks[0][:], x0[:], minus_k_ps[:], ALU.add)
+            else:
+                pe_shifted = held.tile([P, N], F32, name=f"pe_shifted{b}")
+                nc.vector.tensor_tensor(pe_shifted[:], pe_blocks[b][:], minus_k_ps[:], ALU.add)
+                nc.vector.tensor_tensor(y_blocks[b][:], looked_up, pe_shifted[:], ALU.add)
             squared = held.tile([P, N], F32, name=f"squared{b}")
-            nc.scalar.activation(squared[:], centred_blocks[b][:], ACT.Square)
+            nc.scalar.activation(squared[:], y_blocks[b][:], ACT.Square)
             nc.tensor.matmul(
-                var_ps[:], averager[:], squared[:], start=(b == 0), stop=(b == BLOCKS - 1)
+                mean_ps[:], averager[:], y_blocks[b][:], start=(b == 0), stop=(b == BLOCKS - 1)
             )
+            nc.tensor.matmul(var_ps[:], averager[:], squared[:], start=(b == 0), stop=False)
 
+        mean_squared = held.tile([P, N], F32, name="mean_squared")
+        nc.scalar.activation(mean_squared[:], mean_ps[:], ACT.Square)
+        nc.tensor.matmul(var_ps[:], minus_block_averager[:], mean_squared[:], start=False, stop=True)
         rstd = held.tile([P, N], F32, name="rstd")
         nc.scalar.activation(rstd[:], var_ps[:], ACT.Abs_reciprocal_sqrt, bias=EPS)
 
+        centred_blocks = [held.tile([P, N], F32, name=f"centred{b}") for b in range(BLOCKS)]
+        for b in range(BLOCKS):
+            nc.vector.tensor_tensor(centred_blocks[b][:], y_blocks[b][:], mean_ps[:], ALU.subtract)
         for b in range(BLOCKS):
             normed = held.tile([P, N], F32, name=f"normed{b}")
             nc.vector.tensor_tensor(normed[:], centred_blocks[b][:], rstd[:], ALU.mult)

@@ -67,18 +67,24 @@ def tile_decoderlm_kernel(tc, table, pe, gain, bias, offs, out):
             )
             nc.tensor.matmul(var_ps[:], averager[:], squared[:], start=(b == 0), stop=False)
 
+        mean = held.tile([P, N], F32, name="mean")
+        nc.scalar.copy(mean[:], mean_ps[:])
         mean_squared = held.tile([P, N], F32, name="mean_squared")
-        nc.scalar.activation(mean_squared[:], mean_ps[:], ACT.Square)
+        nc.scalar.activation(mean_squared[:], mean[:], ACT.Square)
         nc.tensor.matmul(var_ps[:], minus_block_averager[:], mean_squared[:], start=False, stop=True)
         rstd = held.tile([P, N], F32, name="rstd")
         nc.scalar.activation(rstd[:], var_ps[:], ACT.Abs_reciprocal_sqrt, bias=EPS)
 
         centred_blocks = [held.tile([P, N], F32, name=f"centred{b}") for b in range(BLOCKS)]
         for b in range(BLOCKS):
-            nc.vector.tensor_tensor(centred_blocks[b][:], y_blocks[b][:], mean_ps[:], ALU.subtract)
+            if b % 4 == 3:
+                nc.gpsimd.tensor_tensor(centred_blocks[b][:], y_blocks[b][:], mean[:], ALU.subtract)
+            else:
+                nc.vector.tensor_tensor(centred_blocks[b][:], y_blocks[b][:], mean_ps[:], ALU.subtract)
         for b in range(BLOCKS):
             normed = held.tile([P, N], F32, name=f"normed{b}")
-            nc.vector.tensor_tensor(normed[:], centred_blocks[b][:], rstd[:], ALU.mult)
+            engine = nc.gpsimd if b % 4 == 3 else nc.vector
+            engine.tensor_tensor(normed[:], centred_blocks[b][:], rstd[:], ALU.mult)
             result = held.tile([P, N], F32, name=f"result{b}")
             nc.scalar.activation(
                 result[:],

@@ -10,6 +10,7 @@ P = 128
 C, S, N = 1024, 2048, 512
 BLOCKS = C // P
 EPS = 1e-5
+VECTOR_CENTRES = 5
 
 FLOPS = 8 * C * N
 
@@ -45,6 +46,10 @@ def tile_decoderlm_kernel(tc, table, pe, gain, bias, offs, out):
         minus_block_averager = held.tile([P, P], F32, name="minus_block_averager")
         nc.gpsimd.memset(minus_block_averager[:], -1.0 / P)
 
+        warm = held.tile([P, 1], F32, name="warm")
+        nc.gpsimd.memset(warm[:], 1.0)
+        nc.scalar.activation(warm[:], warm[:], ACT.Abs_reciprocal_sqrt)
+
         minus_k_ps = psum.tile([P, N], F32, name="minus_k_ps")
         mean_ps = psum.tile([P, N], F32, name="mean_ps")
         var_ps = psum.tile([P, N], F32, name="var_ps")
@@ -77,14 +82,13 @@ def tile_decoderlm_kernel(tc, table, pe, gain, bias, offs, out):
 
         centred_blocks = [held.tile([P, N], F32, name=f"centred{b}") for b in range(BLOCKS)]
         for b in range(BLOCKS):
-            if b % 4 == 3:
-                nc.gpsimd.tensor_tensor(centred_blocks[b][:], y_blocks[b][:], mean[:], ALU.subtract)
-            else:
+            if b < VECTOR_CENTRES:
                 nc.vector.tensor_tensor(centred_blocks[b][:], y_blocks[b][:], mean_ps[:], ALU.subtract)
+            else:
+                nc.gpsimd.tensor_tensor(centred_blocks[b][:], y_blocks[b][:], mean[:], ALU.subtract)
         for b in range(BLOCKS):
             normed = held.tile([P, N], F32, name=f"normed{b}")
-            engine = nc.gpsimd if b % 4 == 3 else nc.vector
-            engine.tensor_tensor(normed[:], centred_blocks[b][:], rstd[:], ALU.mult)
+            nc.vector.tensor_tensor(normed[:], centred_blocks[b][:], rstd[:], ALU.mult)
             result = held.tile([P, N], F32, name=f"result{b}")
             nc.scalar.activation(
                 result[:],

@@ -54,6 +54,7 @@ def tile_decoderlm_kernel(tc, table, pe, gain, bias, offs, out):
         mean_ps = psum.tile([P, N], F32, name="mean_ps")
         var_ps = psum.tile([P, N], F32, name="var_ps")
         y_blocks = [held.tile([P, N], F32, name=f"y{b}") for b in range(BLOCKS)]
+        squared_blocks = [held.tile([P, N], F32, name=f"squared{b}") for b in range(BLOCKS)]
         for b in range(BLOCKS):
             looked_up = table_blocks[b][:].indirect(offsets[:])
             if b == 0:
@@ -65,12 +66,14 @@ def tile_decoderlm_kernel(tc, table, pe, gain, bias, offs, out):
                 pe_shifted = held.tile([P, N], F32, name=f"pe_shifted{b}")
                 nc.vector.tensor_tensor(pe_shifted[:], pe_blocks[b][:], minus_k_ps[:], ALU.add)
                 nc.vector.tensor_tensor(y_blocks[b][:], looked_up, pe_shifted[:], ALU.add)
-            squared = held.tile([P, N], F32, name=f"squared{b}")
-            nc.scalar.activation(squared[:], y_blocks[b][:], ACT.Square)
             nc.tensor.matmul(
                 mean_ps[:], averager[:], y_blocks[b][:], start=(b == 0), stop=(b == BLOCKS - 1)
             )
-            nc.tensor.matmul(var_ps[:], averager[:], squared[:], start=(b == 0), stop=False)
+            nc.scalar.activation(squared_blocks[b][:], y_blocks[b][:], ACT.Square)
+            if b % 2 == 1:
+                pair = held.tile([P, N], F32, name=f"pair{b}")
+                nc.vector.tensor_tensor(pair[:], squared_blocks[b - 1][:], squared_blocks[b][:], ALU.add)
+                nc.tensor.matmul(var_ps[:], averager[:], pair[:], start=(b == 1), stop=False)
 
         mean = held.tile([P, N], F32, name="mean")
         nc.scalar.copy(mean[:], mean_ps[:])

@@ -10,7 +10,6 @@ P = 128
 C, S, N = 1024, 2048, 512
 BLOCKS = C // P
 EPS = 1e-5
-VECTOR_CENTRES = 5
 
 FLOPS = 8 * C * N
 
@@ -54,7 +53,6 @@ def tile_decoderlm_kernel(tc, table, pe, gain, bias, offs, out):
         mean_ps = psum.tile([P, N], F32, name="mean_ps")
         var_ps = psum.tile([P, N], F32, name="var_ps")
         y_blocks = [held.tile([P, N], F32, name=f"y{b}") for b in range(BLOCKS)]
-        squared_blocks = [held.tile([P, N], F32, name=f"squared{b}") for b in range(BLOCKS)]
         for b in range(BLOCKS):
             looked_up = table_blocks[b][:].indirect(offsets[:])
             if b == 0:
@@ -66,29 +64,22 @@ def tile_decoderlm_kernel(tc, table, pe, gain, bias, offs, out):
                 pe_shifted = held.tile([P, N], F32, name=f"pe_shifted{b}")
                 nc.vector.tensor_tensor(pe_shifted[:], pe_blocks[b][:], minus_k_ps[:], ALU.add)
                 nc.vector.tensor_tensor(y_blocks[b][:], looked_up, pe_shifted[:], ALU.add)
+            squared = held.tile([P, N], F32, name=f"squared{b}")
+            nc.scalar.activation(squared[:], y_blocks[b][:], ACT.Square)
             nc.tensor.matmul(
                 mean_ps[:], averager[:], y_blocks[b][:], start=(b == 0), stop=(b == BLOCKS - 1)
             )
-            nc.scalar.activation(squared_blocks[b][:], y_blocks[b][:], ACT.Square)
-            if b % 2 == 1:
-                pair = held.tile([P, N], F32, name=f"pair{b}")
-                nc.vector.tensor_tensor(pair[:], squared_blocks[b - 1][:], squared_blocks[b][:], ALU.add)
-                nc.tensor.matmul(var_ps[:], averager[:], pair[:], start=(b == 1), stop=False)
+            nc.tensor.matmul(var_ps[:], averager[:], squared[:], start=(b == 0), stop=False)
 
-        mean = held.tile([P, N], F32, name="mean")
-        nc.scalar.copy(mean[:], mean_ps[:])
         mean_squared = held.tile([P, N], F32, name="mean_squared")
-        nc.scalar.activation(mean_squared[:], mean[:], ACT.Square)
+        nc.scalar.activation(mean_squared[:], mean_ps[:], ACT.Square)
         nc.tensor.matmul(var_ps[:], minus_block_averager[:], mean_squared[:], start=False, stop=True)
         rstd = held.tile([P, N], F32, name="rstd")
         nc.scalar.activation(rstd[:], var_ps[:], ACT.Abs_reciprocal_sqrt, bias=EPS)
 
         centred_blocks = [held.tile([P, N], F32, name=f"centred{b}") for b in range(BLOCKS)]
         for b in range(BLOCKS):
-            if b < VECTOR_CENTRES:
-                nc.vector.tensor_tensor(centred_blocks[b][:], y_blocks[b][:], mean_ps[:], ALU.subtract)
-            else:
-                nc.gpsimd.tensor_tensor(centred_blocks[b][:], y_blocks[b][:], mean[:], ALU.subtract)
+            nc.vector.tensor_tensor(centred_blocks[b][:], y_blocks[b][:], mean_ps[:], ALU.subtract)
         for b in range(BLOCKS):
             normed = held.tile([P, N], F32, name=f"normed{b}")
             nc.vector.tensor_tensor(normed[:], centred_blocks[b][:], rstd[:], ALU.mult)

@@ -10,6 +10,9 @@ P = 128
 C, S, N = 1024, 2048, 512
 BLOCKS = C // P
 EPS = 1e-5
+VECTOR_CENTRES = 5
+PIECES = 2
+PIECE = N // PIECES
 
 FLOPS = 8 * C * N
 
@@ -49,37 +52,66 @@ def tile_decoderlm_kernel(tc, table, pe, gain, bias, offs, out):
         nc.gpsimd.memset(warm[:], 1.0)
         nc.scalar.activation(warm[:], warm[:], ACT.Abs_reciprocal_sqrt)
 
+        cols = [slice(i * PIECE, (i + 1) * PIECE) for i in range(PIECES)]
+        piece_offsets = [offsets[:, i * PIECE // 16 : (i + 1) * PIECE // 16] for i in range(PIECES)]
         minus_k_ps = psum.tile([P, N], F32, name="minus_k_ps")
-        mean_ps = psum.tile([P, N], F32, name="mean_ps")
-        var_ps = psum.tile([P, N], F32, name="var_ps")
+        mean_ps = [psum.tile([P, PIECE], F32, name=f"mean_ps{i}") for i in range(PIECES)]
+        var_ps = [psum.tile([P, PIECE], F32, name=f"var_ps{i}") for i in range(PIECES)]
         y_blocks = [held.tile([P, N], F32, name=f"y{b}") for b in range(BLOCKS)]
         for b in range(BLOCKS):
-            looked_up = table_blocks[b][:].indirect(offsets[:])
             if b == 0:
                 x0 = held.tile([P, N], F32, name="x0")
-                nc.vector.tensor_tensor(x0[:], looked_up, pe_blocks[0][:], ALU.add)
+                for i in range(PIECES):
+                    nc.vector.tensor_tensor(
+                        x0[:, cols[i]],
+                        table_blocks[0][:].indirect(piece_offsets[i]),
+                        pe_blocks[0][:, cols[i]],
+                        ALU.add,
+                    )
                 nc.tensor.matmul(minus_k_ps[:], minus_block_averager[:], x0[:], start=True, stop=True)
                 nc.vector.tensor_tensor(y_blocks[0][:], x0[:], minus_k_ps[:], ALU.add)
             else:
                 pe_shifted = held.tile([P, N], F32, name=f"pe_shifted{b}")
                 nc.vector.tensor_tensor(pe_shifted[:], pe_blocks[b][:], minus_k_ps[:], ALU.add)
-                nc.vector.tensor_tensor(y_blocks[b][:], looked_up, pe_shifted[:], ALU.add)
+                for i in range(PIECES):
+                    nc.vector.tensor_tensor(
+                        y_blocks[b][:, cols[i]],
+                        table_blocks[b][:].indirect(piece_offsets[i]),
+                        pe_shifted[:, cols[i]],
+                        ALU.add,
+                    )
             squared = held.tile([P, N], F32, name=f"squared{b}")
-            nc.scalar.activation(squared[:], y_blocks[b][:], ACT.Square)
-            nc.tensor.matmul(
-                mean_ps[:], averager[:], y_blocks[b][:], start=(b == 0), stop=(b == BLOCKS - 1)
-            )
-            nc.tensor.matmul(var_ps[:], averager[:], squared[:], start=(b == 0), stop=False)
+            for i in range(PIECES):
+                nc.tensor.matmul(
+                    mean_ps[i][:],
+                    averager[:],
+                    y_blocks[b][:, cols[i]],
+                    start=(b == 0),
+                    stop=(b == BLOCKS - 1),
+                )
+                nc.scalar.activation(squared[:, cols[i]], y_blocks[b][:, cols[i]], ACT.Square)
+                nc.tensor.matmul(var_ps[i][:], averager[:], squared[:, cols[i]], start=(b == 0), stop=False)
 
+        mean = held.tile([P, N], F32, name="mean")
         mean_squared = held.tile([P, N], F32, name="mean_squared")
-        nc.scalar.activation(mean_squared[:], mean_ps[:], ACT.Square)
-        nc.tensor.matmul(var_ps[:], minus_block_averager[:], mean_squared[:], start=False, stop=True)
+        for i in range(PIECES):
+            nc.scalar.copy(mean[:, cols[i]], mean_ps[i][:])
+            nc.scalar.activation(mean_squared[:, cols[i]], mean[:, cols[i]], ACT.Square)
+            nc.tensor.matmul(
+                var_ps[i][:], minus_block_averager[:], mean_squared[:, cols[i]], start=False, stop=True
+            )
         rstd = held.tile([P, N], F32, name="rstd")
-        nc.scalar.activation(rstd[:], var_ps[:], ACT.Abs_reciprocal_sqrt, bias=EPS)
+        for i in range(PIECES):
+            nc.scalar.activation(rstd[:, cols[i]], var_ps[i][:], ACT.Abs_reciprocal_sqrt, bias=EPS)
 
         centred_blocks = [held.tile([P, N], F32, name=f"centred{b}") for b in range(BLOCKS)]
-        for b in range(BLOCKS):
-            nc.vector.tensor_tensor(centred_blocks[b][:], y_blocks[b][:], mean_ps[:], ALU.subtract)
+        for i in range(PIECES):
+            for b in range(VECTOR_CENTRES):
+                nc.vector.tensor_tensor(
+                    centred_blocks[b][:, cols[i]], y_blocks[b][:, cols[i]], mean_ps[i][:], ALU.subtract
+                )
+        for b in range(VECTOR_CENTRES, BLOCKS):
+            nc.gpsimd.tensor_tensor(centred_blocks[b][:], y_blocks[b][:], mean[:], ALU.subtract)
         for b in range(BLOCKS):
             normed = held.tile([P, N], F32, name=f"normed{b}")
             nc.vector.tensor_tensor(normed[:], centred_blocks[b][:], rstd[:], ALU.mult)

@@ -9,10 +9,11 @@ ACT = mybir.ActivationFunctionType
 P = 128
 C, S, N = 1024, 2048, 512
 BLOCKS = C // P
+CHUNKS = N // P
 EPS = 1e-5
-VECTOR_CENTRES = 5
-PIECES = 2
-PIECE = N // PIECES
+RECORD = 6
+GROUP = 2
+GROUPS = BLOCKS // GROUP
 
 FLOPS = 8 * C * N
 
@@ -21,106 +22,116 @@ def tile_decoderlm_kernel(tc, table, pe, gain, bias, offs, out):
     nc = tc.nc
     with (
         tc.tile_pool(name="held", bufs=1) as held,
-        tc.psum_pool(name="psum", bufs=1) as psum,
+        tc.psum_pool(name="flipped", bufs=2) as flipped,
+        tc.psum_pool(name="flipped_back", bufs=6) as flipped_back,
     ):
         offsets = held.tile([P, N // 16], U16, name="offsets")
         nc.sync.dma_start(offsets[:], offs)
 
-        pe_blocks = [held.tile([P, N], F32, name=f"pe{b}") for b in range(BLOCKS)]
+        table_by_block = table.rearrange("(p b) s -> b p s", b=BLOCKS)
+        pe_by_partition = pe.rearrange("(p b) n -> p b n", b=BLOCKS)
+        out_by_partition = out.rearrange("(p b) n -> p b n", b=BLOCKS)
+        pe_tile = held.tile([P, BLOCKS, N], F32, name="pe_tile")
         table_blocks = [held.tile([P, S], F32, name=f"table{b}") for b in range(BLOCKS)]
         for b in range(BLOCKS):
-            rows = slice(b * P, (b + 1) * P)
-            nc.sync.dma_start(pe_blocks[b][:], pe[rows, :])
-            nc.sync.dma_start(table_blocks[b][:], table[rows, :])
+            nc.sync.dma_start(pe_tile[:, b, :], pe_by_partition[:, b, :])
+            nc.sync.dma_start(table_blocks[b][:], table_by_block[b])
 
-        affine_rows = held.tile([2 * BLOCKS, P], F32, name="affine_rows")
-        nc.scalar.dma_start(affine_rows[:BLOCKS, :], gain.rearrange("(b p) o -> b (p o)", p=P))
-        nc.scalar.dma_start(affine_rows[BLOCKS:, :], bias.rearrange("(b p) o -> b (p o)", p=P))
-        identity = held.tile([2 * BLOCKS, 2 * BLOCKS], F32, name="identity")
+        gain_tile = held.tile([P, BLOCKS], F32, name="gain_tile")
+        nc.scalar.dma_start(gain_tile[:], gain.rearrange("(p b) o -> p (b o)", b=BLOCKS))
+        bias_tile = held.tile([P, BLOCKS], F32, name="bias_tile")
+        nc.scalar.dma_start(bias_tile[:], bias.rearrange("(p b) o -> p (b o)", b=BLOCKS))
+
+        identity = held.tile([P, P], F32, name="identity")
         masks.make_identity(nc, identity[:])
-        affine_ps = psum.tile([P, 2 * BLOCKS], F32, name="affine_ps")
-        nc.tensor.matmul(affine_ps[:], affine_rows[:], identity[:], start=True, stop=True)
-        affine = held.tile([P, 2 * BLOCKS], F32, name="affine")
-        nc.vector.tensor_copy(affine[:], affine_ps[:])
-
-        averager = held.tile([P, P], F32, name="averager")
-        nc.gpsimd.memset(averager[:], 1.0 / C)
-        minus_block_averager = held.tile([P, P], F32, name="minus_block_averager")
-        nc.gpsimd.memset(minus_block_averager[:], -1.0 / P)
 
         warm = held.tile([P, 1], F32, name="warm")
         nc.gpsimd.memset(warm[:], 1.0)
         nc.scalar.activation(warm[:], warm[:], ACT.Abs_reciprocal_sqrt)
 
-        cols = [slice(i * PIECE, (i + 1) * PIECE) for i in range(PIECES)]
-        piece_offsets = [offsets[:, i * PIECE // 16 : (i + 1) * PIECE // 16] for i in range(PIECES)]
-        minus_k_ps = psum.tile([P, N], F32, name="minus_k_ps")
-        mean_ps = [psum.tile([P, PIECE], F32, name=f"mean_ps{i}") for i in range(PIECES)]
-        var_ps = [psum.tile([P, PIECE], F32, name=f"var_ps{i}") for i in range(PIECES)]
-        y_blocks = [held.tile([P, N], F32, name=f"y{b}") for b in range(BLOCKS)]
-        for b in range(BLOCKS):
-            if b == 0:
-                x0 = held.tile([P, N], F32, name="x0")
-                for i in range(PIECES):
-                    nc.vector.tensor_tensor(
-                        x0[:, cols[i]],
-                        table_blocks[0][:].indirect(piece_offsets[i]),
-                        pe_blocks[0][:, cols[i]],
-                        ALU.add,
-                    )
-                nc.tensor.matmul(minus_k_ps[:], minus_block_averager[:], x0[:], start=True, stop=True)
-                nc.vector.tensor_tensor(y_blocks[0][:], x0[:], minus_k_ps[:], ALU.add)
-            else:
-                pe_shifted = held.tile([P, N], F32, name=f"pe_shifted{b}")
-                nc.vector.tensor_tensor(pe_shifted[:], pe_blocks[b][:], minus_k_ps[:], ALU.add)
-                for i in range(PIECES):
-                    nc.vector.tensor_tensor(
-                        y_blocks[b][:, cols[i]],
-                        table_blocks[b][:].indirect(piece_offsets[i]),
-                        pe_shifted[:, cols[i]],
-                        ALU.add,
-                    )
-            squared = held.tile([P, N], F32, name=f"squared{b}")
-            for i in range(PIECES):
-                nc.tensor.matmul(
-                    mean_ps[i][:],
-                    averager[:],
-                    y_blocks[b][:, cols[i]],
-                    start=(b == 0),
-                    stop=(b == BLOCKS - 1),
-                )
-                nc.scalar.activation(squared[:, cols[i]], y_blocks[b][:, cols[i]], ACT.Square)
-                nc.tensor.matmul(var_ps[i][:], averager[:], squared[:, cols[i]], start=(b == 0), stop=False)
+        x_t = held.tile([P, CHUNKS, C], F32, name="x_t")
+        records = held.tile([P, CHUNKS, BLOCKS * RECORD], F32, name="records")
+        banks = {}
 
-        mean = held.tile([P, N], F32, name="mean")
-        mean_squared = held.tile([P, N], F32, name="mean_squared")
-        for i in range(PIECES):
-            nc.scalar.copy(mean[:, cols[i]], mean_ps[i][:])
-            nc.scalar.activation(mean_squared[:, cols[i]], mean[:, cols[i]], ACT.Square)
-            nc.tensor.matmul(
-                var_ps[i][:], minus_block_averager[:], mean_squared[:, cols[i]], start=False, stop=True
-            )
-        rstd = held.tile([P, N], F32, name="rstd")
-        for i in range(PIECES):
-            nc.scalar.activation(rstd[:, cols[i]], var_ps[i][:], ACT.Abs_reciprocal_sqrt, bias=EPS)
-
-        centred_blocks = [held.tile([P, N], F32, name=f"centred{b}") for b in range(BLOCKS)]
-        for i in range(PIECES):
-            for b in range(VECTOR_CENTRES):
+        def look_up_and_flip(b):
+            x = held.tile([P, N], F32, name=f"x{b}")
+            banks[b] = flipped.tile([P, CHUNKS, P], F32, name="bank")
+            for q in range(CHUNKS):
+                tokens = slice(q * P, (q + 1) * P)
                 nc.vector.tensor_tensor(
-                    centred_blocks[b][:, cols[i]], y_blocks[b][:, cols[i]], mean_ps[i][:], ALU.subtract
+                    x[:, tokens],
+                    table_blocks[b][:].indirect(offsets[:, q * P // 16 : (q + 1) * P // 16]),
+                    pe_tile[:, b, tokens],
+                    ALU.add,
                 )
-        for b in range(VECTOR_CENTRES, BLOCKS):
-            nc.gpsimd.tensor_tensor(centred_blocks[b][:], y_blocks[b][:], mean[:], ALU.subtract)
+                nc.tensor.transpose(banks[b][:, q, :], x[:, tokens], identity[:])
+
+        def record(b, q):
+            nc.vector.bn_stats(records[:, q, b * RECORD : (b + 1) * RECORD], banks[b][:, q, :])
+
+        def keep(b):
+            nc.scalar.copy(x_t[:, :, b * P : (b + 1) * P], banks[b][:])
+
         for b in range(BLOCKS):
-            normed = held.tile([P, N], F32, name=f"normed{b}")
-            nc.vector.tensor_tensor(normed[:], centred_blocks[b][:], rstd[:], ALU.mult)
-            result = held.tile([P, N], F32, name=f"result{b}")
-            nc.scalar.activation(
-                result[:],
-                normed[:],
-                ACT.Identity,
-                scale=affine[:, b : b + 1],
-                bias=affine[:, BLOCKS + b : BLOCKS + b + 1],
-            )
-            nc.sync.dma_start(out[b * P : (b + 1) * P, :], result[:])
+            look_up_and_flip(b)
+            if b > 0:
+                for q in range(CHUNKS):
+                    record(b - 1, q)
+                keep(b - 1)
+
+        mean_var = held.tile([P, CHUNKS, 2], F32, name="mean_var")
+        rstd = held.tile([P, CHUNKS], F32, name="rstd")
+        for q in range(CHUNKS):
+            record(BLOCKS - 1, q)
+        for q in range(CHUNKS):
+            nc.vector.bn_aggr(mean_var[:, q, :], records[:, q, :])
+        nc.scalar.activation(rstd[:], mean_var[:, :, 1], ACT.Abs_reciprocal_sqrt, bias=EPS)
+        keep(BLOCKS - 1)
+
+        normed_t = held.tile([P, CHUNKS, C], F32, name="normed_t")
+        result = held.tile([P, BLOCKS, N], F32, name="result")
+
+        def normalise(g):
+            channels = slice(g * GROUP * P, (g + 1) * GROUP * P)
+            for q in range(CHUNKS):
+                nc.vector.tensor_scalar(
+                    normed_t[:, q, channels],
+                    x_t[:, q, channels],
+                    mean_var[:, q, 0:1],
+                    rstd[:, q : q + 1],
+                    ALU.subtract,
+                    ALU.mult,
+                )
+
+        normalise(0)
+        for g in range(GROUPS):
+            banks_back = {}
+            for b in range(g * GROUP, (g + 1) * GROUP):
+                banks_back[b] = flipped_back.tile([P, N], F32, name="bank_back")
+                for q in range(CHUNKS):
+                    nc.tensor.transpose(
+                        banks_back[b][:, q * P : (q + 1) * P],
+                        normed_t[:, q, b * P : (b + 1) * P],
+                        identity[:],
+                    )
+            if g + 1 < GROUPS:
+                normalise(g + 1)
+            for b in range(g * GROUP, (g + 1) * GROUP):
+                if b % 4 == 3:
+                    nc.vector.tensor_scalar(
+                        result[:, b, :],
+                        banks_back[b][:],
+                        gain_tile[:, b : b + 1],
+                        bias_tile[:, b : b + 1],
+                        ALU.mult,
+                        ALU.add,
+                    )
+                else:
+                    nc.scalar.activation(
+                        result[:, b, :],
+                        banks_back[b][:],
+                        ACT.Identity,
+                        scale=gain_tile[:, b : b + 1],
+                        bias=bias_tile[:, b : b + 1],
+                    )
+                nc.sync.dma_start(out_by_partition[:, b, :], result[:, b, :])

@@ -22,8 +22,8 @@ def tile_decoderlm_kernel(tc, table, pe, gain, bias, offs, out):
     nc = tc.nc
     with (
         tc.tile_pool(name="held", bufs=1) as held,
-        tc.psum_pool(name="flipped", bufs=2) as flipped,
-        tc.psum_pool(name="flipped_back", bufs=6) as flipped_back,
+        tc.psum_pool(name="flipped", bufs=4) as flipped,
+        tc.psum_pool(name="flipped_back", bufs=4) as flipped_back,
     ):
         offsets = held.tile([P, N // 16], U16, name="offsets")
         nc.sync.dma_start(offsets[:], offs)
@@ -55,8 +55,9 @@ def tile_decoderlm_kernel(tc, table, pe, gain, bias, offs, out):
 
         def look_up_and_flip(b):
             x = held.tile([P, N], F32, name=f"x{b}")
-            banks[b] = flipped.tile([P, CHUNKS, P], F32, name="bank")
             for q in range(CHUNKS):
+                if q % 2 == 0:
+                    banks[b, q // 2] = flipped.tile([P, 2, P], F32, name="bank")
                 tokens = slice(q * P, (q + 1) * P)
                 nc.vector.tensor_tensor(
                     x[:, tokens],
@@ -64,29 +65,28 @@ def tile_decoderlm_kernel(tc, table, pe, gain, bias, offs, out):
                     pe_tile[:, b, tokens],
                     ALU.add,
                 )
-                nc.tensor.transpose(banks[b][:, q, :], x[:, tokens], identity[:])
+                nc.tensor.transpose(banks[b, q // 2][:, q % 2, :], x[:, tokens], identity[:])
 
         def record(b, q):
-            nc.vector.bn_stats(records[:, q, b * RECORD : (b + 1) * RECORD], banks[b][:, q, :])
+            nc.vector.bn_stats(
+                records[:, q, b * RECORD : (b + 1) * RECORD], banks[b, q // 2][:, q % 2, :]
+            )
 
         def keep(b):
-            nc.scalar.copy(x_t[:, :, b * P : (b + 1) * P], banks[b][:])
+            for h in range(CHUNKS // 2):
+                nc.scalar.copy(x_t[:, 2 * h : 2 * h + 2, b * P : (b + 1) * P], banks[b, h][:])
 
         for b in range(BLOCKS):
             look_up_and_flip(b)
-            if b > 0:
-                for q in range(CHUNKS):
-                    record(b - 1, q)
-                keep(b - 1)
+            for q in range(CHUNKS):
+                record(b, q)
+            keep(b)
 
         mean_var = held.tile([P, CHUNKS, 2], F32, name="mean_var")
         rstd = held.tile([P, CHUNKS], F32, name="rstd")
         for q in range(CHUNKS):
-            record(BLOCKS - 1, q)
-        for q in range(CHUNKS):
             nc.vector.bn_aggr(mean_var[:, q, :], records[:, q, :])
         nc.scalar.activation(rstd[:], mean_var[:, :, 1], ACT.Abs_reciprocal_sqrt, bias=EPS)
-        keep(BLOCKS - 1)
 
         normed_t = held.tile([P, CHUNKS, C], F32, name="normed_t")
         result = held.tile([P, BLOCKS, N], F32, name="result")

@@ -56,8 +56,7 @@ def tile_decoderlm_kernel(tc, table, pe, gain, bias, offs, out):
         def look_up_and_flip(b):
             x = held.tile([P, N], F32, name=f"x{b}")
             for q in range(CHUNKS):
-                if q % 2 == 0:
-                    banks[b, q // 2] = flipped.tile([P, 2, P], F32, name="bank")
+                banks[b, q] = flipped.tile([P, P], F32, name="bank")
                 tokens = slice(q * P, (q + 1) * P)
                 nc.vector.tensor_tensor(
                     x[:, tokens],
@@ -65,16 +64,14 @@ def tile_decoderlm_kernel(tc, table, pe, gain, bias, offs, out):
                     pe_tile[:, b, tokens],
                     ALU.add,
                 )
-                nc.tensor.transpose(banks[b, q // 2][:, q % 2, :], x[:, tokens], identity[:])
+                nc.tensor.transpose(banks[b, q][:], x[:, tokens], identity[:])
 
         def record(b, q):
-            nc.vector.bn_stats(
-                records[:, q, b * RECORD : (b + 1) * RECORD], banks[b, q // 2][:, q % 2, :]
-            )
+            nc.vector.bn_stats(records[:, q, b * RECORD : (b + 1) * RECORD], banks[b, q][:])
 
         def keep(b):
-            for h in range(CHUNKS // 2):
-                nc.scalar.copy(x_t[:, 2 * h : 2 * h + 2, b * P : (b + 1) * P], banks[b, h][:])
+            for q in range(CHUNKS):
+                nc.scalar.copy(x_t[:, q, b * P : (b + 1) * P], banks[b, q][:])
 
         for b in range(BLOCKS):
             look_up_and_flip(b)
@@ -86,7 +83,10 @@ def tile_decoderlm_kernel(tc, table, pe, gain, bias, offs, out):
         rstd = held.tile([P, CHUNKS], F32, name="rstd")
         for q in range(CHUNKS):
             nc.vector.bn_aggr(mean_var[:, q, :], records[:, q, :])
-        nc.scalar.activation(rstd[:], mean_var[:, :, 1], ACT.Abs_reciprocal_sqrt, bias=EPS)
+        for q in range(CHUNKS):
+            nc.scalar.activation(
+                rstd[:, q : q + 1], mean_var[:, q, 1:2], ACT.Abs_reciprocal_sqrt, bias=EPS
+            )
 
         normed_t = held.tile([P, CHUNKS, C], F32, name="normed_t")
         result = held.tile([P, BLOCKS, N], F32, name="result")

@@ -33,9 +33,12 @@ def tile_decoderlm_kernel(tc, table, pe, gain, bias, offs, out):
         out_by_partition = out.rearrange("(p b) n -> p b n", b=BLOCKS)
         pe_tile = held.tile([P, BLOCKS, N], F32, name="pe_tile")
         table_blocks = [held.tile([P, S], F32, name=f"table{b}") for b in range(BLOCKS)]
-        for b in range(BLOCKS):
-            nc.sync.dma_start(pe_tile[:, b, :], pe_by_partition[:, b, :])
-            nc.sync.dma_start(table_blocks[b][:], table_by_block[b])
+        for first in range(0, BLOCKS, 2):
+            nc.sync.dma_start(
+                pe_tile[:, first : first + 2, :], pe_by_partition[:, first : first + 2, :]
+            )
+            for b in (first, first + 1):
+                nc.sync.dma_start(table_blocks[b][:], table_by_block[b])
 
         gain_tile = held.tile([P, BLOCKS], F32, name="gain_tile")
         nc.scalar.dma_start(gain_tile[:], gain.rearrange("(p b) o -> p (b o)", b=BLOCKS))

@@ -12,6 +12,8 @@ BLOCKS = C // P
 CHUNKS = N // P
 EPS = 1e-5
 RECORD = 6
+MERGED = 3
+EARLY = BLOCKS - 2
 GROUP = 2
 GROUPS = BLOCKS // GROUP
 
@@ -53,7 +55,9 @@ def tile_decoderlm_kernel(tc, table, pe, gain, bias, offs, out):
         nc.scalar.activation(warm[:], warm[:], ACT.Abs_reciprocal_sqrt)
 
         x_t = held.tile([P, CHUNKS, C], F32, name="x_t")
-        records = held.tile([P, CHUNKS, BLOCKS * RECORD], F32, name="records")
+        early_records = held.tile([P, CHUNKS, EARLY * RECORD], F32, name="early_records")
+        records = held.tile([P, CHUNKS, MERGED + (BLOCKS - EARLY) * RECORD], F32, name="records")
+        nc.vector.memset(records[:, :, 0:1], float(EARLY * P))
         banks = {}
 
         def look_up_and_flip(b):
@@ -70,7 +74,19 @@ def tile_decoderlm_kernel(tc, table, pe, gain, bias, offs, out):
                 nc.tensor.transpose(banks[b, q][:], x[:, tokens], identity[:])
 
         def record(b, q):
-            nc.vector.bn_stats(records[:, q, b * RECORD : (b + 1) * RECORD], banks[b, q][:])
+            if b < EARLY:
+                place = early_records[:, q, b * RECORD : (b + 1) * RECORD]
+            else:
+                first = MERGED + (b - EARLY) * RECORD
+                place = records[:, q, first : first + RECORD]
+            nc.vector.bn_stats(place, banks[b, q][:])
+
+        def merge_early_records():
+            for q in range(CHUNKS):
+                nc.vector.bn_aggr(records[:, q, 1:3], early_records[:, q, :])
+            nc.vector.tensor_scalar(
+                records[:, :, 2:3], records[:, :, 2:3], float(EARLY * P), None, ALU.mult
+            )
 
         def keep(b):
             for q in range(CHUNKS):
@@ -81,6 +97,8 @@ def tile_decoderlm_kernel(tc, table, pe, gain, bias, offs, out):
             for q in range(CHUNKS):
                 record(b, q)
             keep(b)
+            if b == EARLY - 1:
+                merge_early_records()
 
         mean_var = held.tile([P, CHUNKS, 2], F32, name="mean_var")
         rstd = held.tile([P, CHUNKS], F32, name="rstd")

@@ -54,7 +54,7 @@ def tile_decoderlm_kernel(tc, table, pe, gain, bias, offs, out):
         nc.gpsimd.memset(warm[:], 1.0)
         nc.scalar.activation(warm[:], warm[:], ACT.Abs_reciprocal_sqrt)
 
-        x_t = held.tile([P, CHUNKS, C], F32, name="x_t")
+        x_t = held.tile([P, CHUNKS, C - P], F32, name="x_t")
         early_records = held.tile([P, CHUNKS, EARLY * RECORD], F32, name="early_records")
         records = held.tile([P, CHUNKS, MERGED + (BLOCKS - EARLY) * RECORD], F32, name="records")
         nc.vector.memset(records[:, :, 0:1], float(EARLY * P))
@@ -96,7 +96,8 @@ def tile_decoderlm_kernel(tc, table, pe, gain, bias, offs, out):
             look_up_and_flip(b)
             for q in range(CHUNKS):
                 record(b, q)
-            keep(b)
+            if b < BLOCKS - 1:
+                keep(b)
             if b == EARLY - 1:
                 merge_early_records()
 
@@ -112,17 +113,23 @@ def tile_decoderlm_kernel(tc, table, pe, gain, bias, offs, out):
         normed_t = held.tile([P, CHUNKS, C], F32, name="normed_t")
         result = held.tile([P, BLOCKS, N], F32, name="result")
 
+        def normalise_piece(q, first, last, source):
+            nc.vector.tensor_scalar(
+                normed_t[:, q, first * P : last * P],
+                source,
+                mean_var[:, q, 0:1],
+                rstd[:, q : q + 1],
+                ALU.subtract,
+                ALU.mult,
+            )
+
         def normalise(g):
-            channels = slice(g * GROUP * P, (g + 1) * GROUP * P)
+            first, last = g * GROUP, (g + 1) * GROUP
+            kept = min(last, BLOCKS - 1)
             for q in range(CHUNKS):
-                nc.vector.tensor_scalar(
-                    normed_t[:, q, channels],
-                    x_t[:, q, channels],
-                    mean_var[:, q, 0:1],
-                    rstd[:, q : q + 1],
-                    ALU.subtract,
-                    ALU.mult,
-                )
+                normalise_piece(q, first, kept, x_t[:, q, first * P : kept * P])
+                if last == BLOCKS:
+                    normalise_piece(q, kept, last, banks[kept, q][:])
 
         normalise(0)
         for g in range(GROUPS):

@@ -145,7 +145,7 @@ def tile_decoderlm_kernel(tc, table, pe, gain, bias, offs, out):
             if g + 1 < GROUPS:
                 normalise(g + 1)
             for b in range(g * GROUP, (g + 1) * GROUP):
-                if b % 4 == 3:
+                if b % 4 == 1:
                     nc.vector.tensor_scalar(
                         result[:, b, :],
                         banks_back[b][:],

@@ -43,9 +43,9 @@ def tile_decoderlm_kernel(tc, table, pe, gain, bias, offs, out):
                 nc.sync.dma_start(table_blocks[b][:], table_by_block[b])
 
         gain_tile = held.tile([P, BLOCKS], F32, name="gain_tile")
-        nc.scalar.dma_start(gain_tile[:], gain.rearrange("(p b) o -> p (b o)", b=BLOCKS))
+        nc.sync.dma_start(gain_tile[:], gain.rearrange("(p b) o -> p (b o)", b=BLOCKS))
         bias_tile = held.tile([P, BLOCKS], F32, name="bias_tile")
-        nc.scalar.dma_start(bias_tile[:], bias.rearrange("(p b) o -> p (b o)", b=BLOCKS))
+        nc.sync.dma_start(bias_tile[:], bias.rearrange("(p b) o -> p (b o)", b=BLOCKS))
 
         identity = held.tile([P, P], F32, name="identity")
         masks.make_identity(nc, identity[:])

@@ -13,6 +13,7 @@ CHUNKS = N // P
 EPS = 1e-5
 RECORD = 6
 MERGED = 3
+FIRST = BLOCKS - 4
 EARLY = BLOCKS - 2
 GROUP = 2
 GROUPS = BLOCKS // GROUP
@@ -31,16 +32,17 @@ def tile_decoderlm_kernel(tc, table, pe, gain, bias, offs, out):
         nc.sync.dma_start(offsets[:], offs)
 
         table_by_block = table.rearrange("(p b) s -> b p s", b=BLOCKS)
-        pe_by_partition = pe.rearrange("(p b) n -> p b n", b=BLOCKS)
+        pe_by_partition = pe.rearrange("(p b) n -> p (b n)", b=BLOCKS)
         out_by_partition = out.rearrange("(p b) n -> p b n", b=BLOCKS)
-        pe_tile = held.tile([P, BLOCKS, N], F32, name="pe_tile")
+        pe_tile = held.tile([P, BLOCKS * N], F32, name="pe_tile")
         table_blocks = [held.tile([P, S], F32, name=f"table{b}") for b in range(BLOCKS)]
+        late = (BLOCKS - 1) * N + P
         for first in range(0, BLOCKS, 2):
-            nc.sync.dma_start(
-                pe_tile[:, first : first + 2, :], pe_by_partition[:, first : first + 2, :]
-            )
+            columns = slice(first * N, min((first + 2) * N, late))
+            nc.sync.dma_start(pe_tile[:, columns], pe_by_partition[:, columns])
             for b in (first, first + 1):
                 nc.sync.dma_start(table_blocks[b][:], table_by_block[b])
+        nc.sync.dma_start(pe_tile[:, late:], pe_by_partition[:, late:])
 
         gain_tile = held.tile([P, BLOCKS], F32, name="gain_tile")
         nc.sync.dma_start(gain_tile[:], gain.rearrange("(p b) o -> p (b o)", b=BLOCKS))
@@ -55,8 +57,10 @@ def tile_decoderlm_kernel(tc, table, pe, gain, bias, offs, out):
         nc.scalar.activation(warm[:], warm[:], ACT.Abs_reciprocal_sqrt)
 
         x_t = held.tile([P, CHUNKS, C - P], F32, name="x_t")
-        early_records = held.tile([P, CHUNKS, EARLY * RECORD], F32, name="early_records")
+        first_records = held.tile([P, CHUNKS, FIRST * RECORD], F32, name="first_records")
+        early_records = held.tile([P, CHUNKS, MERGED + (EARLY - FIRST) * RECORD], F32, name="early_records")
         records = held.tile([P, CHUNKS, MERGED + (BLOCKS - EARLY) * RECORD], F32, name="records")
+        nc.vector.memset(early_records[:, :, 0:1], float(FIRST * P))
         nc.vector.memset(records[:, :, 0:1], float(EARLY * P))
         banks = {}
 
@@ -68,24 +72,27 @@ def tile_decoderlm_kernel(tc, table, pe, gain, bias, offs, out):
                 nc.vector.tensor_tensor(
                     x[:, tokens],
                     table_blocks[b][:].indirect(offsets[:, q * P // 16 : (q + 1) * P // 16]),
-                    pe_tile[:, b, tokens],
+                    pe_tile[:, b * N + q * P : b * N + (q + 1) * P],
                     ALU.add,
                 )
                 nc.tensor.transpose(banks[b, q][:], x[:, tokens], identity[:])
 
         def record(b, q):
-            if b < EARLY:
-                place = early_records[:, q, b * RECORD : (b + 1) * RECORD]
+            if b < FIRST:
+                place = first_records[:, q, b * RECORD : (b + 1) * RECORD]
+            elif b < EARLY:
+                first = MERGED + (b - FIRST) * RECORD
+                place = early_records[:, q, first : first + RECORD]
             else:
                 first = MERGED + (b - EARLY) * RECORD
                 place = records[:, q, first : first + RECORD]
             nc.vector.bn_stats(place, banks[b, q][:])
 
-        def merge_early_records():
+        def merge(source, target, blocks):
             for q in range(CHUNKS):
-                nc.vector.bn_aggr(records[:, q, 1:3], early_records[:, q, :])
+                nc.vector.bn_aggr(target[:, q, 1:3], source[:, q, :])
             nc.vector.tensor_scalar(
-                records[:, :, 2:3], records[:, :, 2:3], float(EARLY * P), None, ALU.mult
+                target[:, :, 2:3], target[:, :, 2:3], float(blocks * P), None, ALU.mult
             )
 
         def keep(b):
@@ -98,8 +105,10 @@ def tile_decoderlm_kernel(tc, table, pe, gain, bias, offs, out):
                 record(b, q)
             if b < BLOCKS - 1:
                 keep(b)
+            if b == FIRST - 1:
+                merge(first_records, early_records, FIRST)
             if b == EARLY - 1:
-                merge_early_records()
+                merge(early_records, records, EARLY)
 
         mean_var = held.tile([P, CHUNKS, 2], F32, name="mean_var")
         rstd = held.tile([P, CHUNKS], F32, name="rstd")

import concourse.masks as masks
import concourse.mybir as mybir

F32 = mybir.dt.float32
U16 = mybir.dt.uint16
ALU = mybir.AluOpType
ACT = mybir.ActivationFunctionType

P = 128
C, S, N = 1024, 2048, 512
BLOCKS = C // P
CHUNKS = N // P
EPS = 1e-5
RECORD = 6
MERGED = 3
FIRST = BLOCKS - 4
EARLY = BLOCKS - 2
GROUP = 2
GROUPS = BLOCKS // GROUP

FLOPS = 8 * C * N


def tile_decoderlm_kernel(tc, table, pe, gain, bias, offs, out):
    nc = tc.nc
    with (
        tc.tile_pool(name="held", bufs=1) as held,
        tc.psum_pool(name="flipped", bufs=4) as flipped,
        tc.psum_pool(name="flipped_back", bufs=4) as flipped_back,
    ):
        offsets = held.tile([P, N // 16], U16, name="offsets")
        nc.sync.dma_start(offsets[:], offs)

        table_by_block = table.rearrange("(p b) s -> b p s", b=BLOCKS)
        pe_by_partition = pe.rearrange("(p b) n -> p (b n)", b=BLOCKS)
        out_by_partition = out.rearrange("(p b) n -> p b n", b=BLOCKS)
        pe_tile = held.tile([P, BLOCKS * N], F32, name="pe_tile")
        table_blocks = [held.tile([P, S], F32, name=f"table{b}") for b in range(BLOCKS)]
        late = (BLOCKS - 1) * N + P
        for first in range(0, BLOCKS, 2):
            columns = slice(first * N, min((first + 2) * N, late))
            nc.sync.dma_start(pe_tile[:, columns], pe_by_partition[:, columns])
            for b in (first, first + 1):
                nc.sync.dma_start(table_blocks[b][:], table_by_block[b])
        nc.sync.dma_start(pe_tile[:, late:], pe_by_partition[:, late:])

        gain_tile = held.tile([P, BLOCKS], F32, name="gain_tile")
        nc.sync.dma_start(gain_tile[:], gain.rearrange("(p b) o -> p (b o)", b=BLOCKS))
        bias_tile = held.tile([P, BLOCKS], F32, name="bias_tile")
        nc.sync.dma_start(bias_tile[:], bias.rearrange("(p b) o -> p (b o)", b=BLOCKS))

        identity = held.tile([P, P], F32, name="identity")
        masks.make_identity(nc, identity[:])

        warm = held.tile([P, 1], F32, name="warm")
        nc.gpsimd.memset(warm[:], 1.0)
        nc.scalar.activation(warm[:], warm[:], ACT.Abs_reciprocal_sqrt)

        x_t = held.tile([P, CHUNKS, C - P], F32, name="x_t")
        first_records = held.tile([P, CHUNKS, FIRST * RECORD], F32, name="first_records")
        early_records = held.tile([P, CHUNKS, MERGED + (EARLY - FIRST) * RECORD], F32, name="early_records")
        records = held.tile([P, CHUNKS, MERGED + (BLOCKS - EARLY) * RECORD], F32, name="records")
        nc.vector.memset(early_records[:, :, 0:1], float(FIRST * P))
        nc.vector.memset(records[:, :, 0:1], float(EARLY * P))
        banks = {}

        def look_up_and_flip(b):
            x = held.tile([P, N], F32, name=f"x{b}")
            for q in range(CHUNKS):
                banks[b, q] = flipped.tile([P, P], F32, name="bank")
                tokens = slice(q * P, (q + 1) * P)
                nc.vector.tensor_tensor(
                    x[:, tokens],
                    table_blocks[b][:].indirect(offsets[:, q * P // 16 : (q + 1) * P // 16]),
                    pe_tile[:, b * N + q * P : b * N + (q + 1) * P],
                    ALU.add,
                )
                nc.tensor.transpose(banks[b, q][:], x[:, tokens], identity[:])

        def record(b, q):
            if b < FIRST:
                place = first_records[:, q, b * RECORD : (b + 1) * RECORD]
            elif b < EARLY:
                first = MERGED + (b - FIRST) * RECORD
                place = early_records[:, q, first : first + RECORD]
            else:
                first = MERGED + (b - EARLY) * RECORD
                place = records[:, q, first : first + RECORD]
            nc.vector.bn_stats(place, banks[b, q][:])

        def merge(source, target, blocks):
            for q in range(CHUNKS):
                nc.vector.bn_aggr(target[:, q, 1:3], source[:, q, :])
            nc.vector.tensor_scalar(
                target[:, :, 2:3], target[:, :, 2:3], float(blocks * P), None, ALU.mult
            )

        def keep(b):
            for q in range(CHUNKS):
                nc.scalar.copy(x_t[:, q, b * P : (b + 1) * P], banks[b, q][:])

        for b in range(BLOCKS):
            look_up_and_flip(b)
            for q in range(CHUNKS):
                record(b, q)
            if b < BLOCKS - 1:
                keep(b)
            if b == FIRST - 1:
                merge(first_records, early_records, FIRST)
            if b == EARLY - 1:
                merge(early_records, records, EARLY)

        mean_var = held.tile([P, CHUNKS, 2], F32, name="mean_var")
        rstd = held.tile([P, CHUNKS], F32, name="rstd")
        for q in range(CHUNKS):
            nc.vector.bn_aggr(mean_var[:, q, :], records[:, q, :])
        for q in range(CHUNKS):
            nc.scalar.activation(
                rstd[:, q : q + 1], mean_var[:, q, 1:2], ACT.Abs_reciprocal_sqrt, bias=EPS
            )

        normed_t = held.tile([P, CHUNKS, C], F32, name="normed_t")
        result = held.tile([P, BLOCKS, N], F32, name="result")

        def normalise_piece(q, first, last, source):
            nc.vector.tensor_scalar(
                normed_t[:, q, first * P : last * P],
                source,
                mean_var[:, q, 0:1],
                rstd[:, q : q + 1],
                ALU.subtract,
                ALU.mult,
            )

        def normalise(g):
            first, last = g * GROUP, (g + 1) * GROUP
            kept = min(last, BLOCKS - 1)
            for q in range(CHUNKS):
                normalise_piece(q, first, kept, x_t[:, q, first * P : kept * P])
                if last == BLOCKS:
                    normalise_piece(q, kept, last, banks[kept, q][:])

        normalise(0)
        for g in range(GROUPS):
            banks_back = {}
            for b in range(g * GROUP, (g + 1) * GROUP):
                banks_back[b] = flipped_back.tile([P, N], F32, name="bank_back")
                for q in range(CHUNKS):
                    nc.tensor.transpose(
                        banks_back[b][:, q * P : (q + 1) * P],
                        normed_t[:, q, b * P : (b + 1) * P],
                        identity[:],
                    )
            if g + 1 < GROUPS:
                normalise(g + 1)
            for b in range(g * GROUP, (g + 1) * GROUP):
                if b % 4 == 1:
                    nc.vector.tensor_scalar(
                        result[:, b, :],
                        banks_back[b][:],
                        gain_tile[:, b : b + 1],
                        bias_tile[:, b : b + 1],
                        ALU.mult,
                        ALU.add,
                    )
                else:
                    nc.scalar.activation(
                        result[:, b, :],
                        banks_back[b][:],
                        ACT.Identity,
                        scale=gain_tile[:, b : b + 1],
                        bias=bias_tile[:, b : b + 1],
                    )
                nc.sync.dma_start(out_by_partition[:, b, :], result[:, b, :])
